import numpy as np
import ml_dtypes

BF16 = ml_dtypes.bfloat16


def bf(x):
    return np.asarray(x, np.float32).astype(BF16)


def f32(x):
    return np.asarray(x, np.float32)


def f64(x):
    return np.asarray(x).astype(np.float64)


def striped(idx):
    return np.tile(idx.reshape(-1, 16).T, (8, 1))


D, R, C, S, H, K, N = 128, 3, 512, 512, 256, 8, 2048
EPS = 1e-8


def sigmoid(v):
    return 1.0 / (1.0 + np.exp(-v))


def setup_inputs():
    return {
        'x': f32(0.7 * np.random.standard_normal((C, S))),
        'other': f32(0.7 * np.random.standard_normal((C, N))),
        'w_norm': bf(np.random.standard_normal((D, D)) / np.sqrt(2.0 * D)),
        'b_scalar': f32(0.1 * np.random.standard_normal((D, 1))),
        'w_gate': bf(np.random.standard_normal((D, D)) / np.sqrt(D)),
        'b_gate': f32(0.1 * np.random.standard_normal((D, 1))),
        'offs': striped(np.concatenate([np.random.permutation(S)[:H] for _ in range(K)])),
    }


def reference(x, other, w_norm, b_scalar, w_gate, b_gate, offs):
    idx = offs[:16].T.reshape(-1)
    a = f64(x)[:, idx] + f64(other)
    sp = a[:D]
    vh = a[D:].reshape(R, D, N)
    vn = np.sqrt((vh * vh).sum(axis=0) + EPS)
    s_out = sp + f64(w_norm).T @ vn + f64(b_scalar)
    gate = sigmoid(f64(w_gate).T @ s_out + f64(b_gate))
    return np.concatenate([np.maximum(s_out, 0.0), (vh * gate[None]).reshape(R * D, N)], axis=0)

@@ -1,0 +1,84 @@
+import concourse.mybir as mybir
+from concourse.masks import make_identity
+
+F32, BF16, U16 = mybir.dt.float32, mybir.dt.bfloat16, mybir.dt.uint16
+ADD, MULT = mybir.AluOpType.add, mybir.AluOpType.mult
+ACT = mybir.ActivationFunctionType
+
+P = 128
+BLOCKS = 4
+NODES = 512
+EDGES = 2048
+CHUNK = 512
+EPS = 1e-8
+
+FLOPS = 2 * 2 * P * P * EDGES
+
+
+def tile_messagefunction_kernel(tc, x, other, w_norm, b_scalar, w_gate, b_gate, offs, out):
+    nc = tc.nc
+    with (
+        tc.tile_pool(name="held", bufs=1) as held,
+        tc.tile_pool(name="work", bufs=2) as work,
+        tc.psum_pool(name="psum", bufs=2) as psum,
+    ):
+        offsets = held.tile([P, EDGES // 16], U16, name="offsets")
+        nc.sync.dma_start(offsets[:], offs)
+
+        tables = [held.tile([P, NODES], F32, name=f"table{b}") for b in range(BLOCKS)]
+        for b in range(BLOCKS):
+            nc.sync.dma_start(tables[b][:], x[b * P : (b + 1) * P, :])
+
+        norm_weights = held.tile([P, P], BF16, name="norm_weights")
+        gate_weights = held.tile([P, P], BF16, name="gate_weights")
+        scalar_bias = held.tile([P, 1], F32, name="scalar_bias")
+        gate_bias = held.tile([P, 1], F32, name="gate_bias")
+        nc.sync.dma_start(norm_weights[:], w_norm)
+        nc.sync.dma_start(gate_weights[:], w_gate)
+        nc.sync.dma_start(scalar_bias[:], b_scalar)
+        nc.sync.dma_start(gate_bias[:], b_gate)
+
+        identity = held.tile([P, P], F32, name="identity")
+        make_identity(nc, identity[:])
+        eps = held.tile([P, 1], F32, name="eps")
+        nc.gpsimd.memset(eps[:], EPS)
+
+        for c in range(EDGES // CHUNK):
+            edges = slice(c * CHUNK, (c + 1) * CHUNK)
+            piece = offsets[:, c * CHUNK // 16 : (c + 1) * CHUNK // 16]
+
+            summed = []
+            for b in range(BLOCKS):
+                term = work.tile([P, CHUNK], F32, name=f"term{b}")
+                nc.sync.dma_start(term[:], other[b * P : (b + 1) * P, edges])
+                a = work.tile([P, CHUNK], F32, name=f"a{b}")
+                nc.vector.tensor_tensor(a[:], tables[b][:].indirect(piece), term[:], ADD)
+                summed.append(a)
+            sp, vh = summed[0], summed[1:]
+
+            norm2 = psum.tile([P, CHUNK], F32, name="norm2")
+            for r in range(3):
+                squared = work.tile([P, CHUNK], F32, name=f"squared{r}")
+                nc.scalar.activation(squared[:], vh[r][:], ACT.Square)
+                nc.tensor.matmul(norm2[:], identity[:], squared[:], start=(r == 0), stop=(r == 2))
+            vn = work.tile([P, CHUNK], BF16, name="vn")
+            nc.scalar.activation(vn[:], norm2[:], ACT.Sqrt, bias=eps[:])
+
+            s_psum = psum.tile([P, CHUNK], F32, name="s_psum")
+            nc.tensor.matmul(s_psum[:], norm_weights[:], vn[:], start=True, stop=False)
+            nc.tensor.matmul(s_psum[:], identity[:], sp[:], start=False, stop=True)
+            s_bf16 = work.tile([P, CHUNK], BF16, name="s_bf16")
+            nc.scalar.activation(s_bf16[:], s_psum[:], ACT.Identity, bias=scalar_bias[:])
+            s_relu = work.tile([P, CHUNK], F32, name="s_relu")
+            nc.scalar.activation(s_relu[:], s_psum[:], ACT.Relu, bias=scalar_bias[:])
+            nc.sync.dma_start(out[0:P, edges], s_relu[:])
+
+            gate_psum = psum.tile([P, CHUNK], F32, name="gate_psum")
+            nc.tensor.matmul(gate_psum[:], gate_weights[:], s_bf16[:], start=True, stop=True)
+            gate = work.tile([P, CHUNK], F32, name="gate")
+            nc.scalar.activation(gate[:], gate_psum[:], ACT.Sigmoid, bias=gate_bias[:])
+
+            for r in range(3):
+                gated = work.tile([P, CHUNK], F32, name=f"gated{r}")
+                nc.gpsimd.tensor_tensor(gated[:], vh[r][:], gate[:], MULT)
+                nc.sync.dma_start(out[(1 + r) * P : (2 + r) * P, edges], gated[:])

@@ -6,10 +6,11 @@ ADD, MULT = mybir.AluOpType.add, mybir.AluOpType.mult
 ACT = mybir.ActivationFunctionType
 
 P = 128
-BLOCKS = 4
 NODES = 512
 EDGES = 2048
 CHUNK = 512
+CHUNKS = EDGES // CHUNK
+GROUP = 2
 EPS = 1e-8
 
 FLOPS = 2 * 2 * P * P * EDGES
@@ -19,66 +20,70 @@ def tile_messagefunction_kernel(tc, x, other, w_norm, b_scalar, w_gate, b_gate, 
     nc = tc.nc
     with (
         tc.tile_pool(name="held", bufs=1) as held,
+        tc.tile_pool(name="per_chunk", bufs=CHUNKS) as per_chunk,
         tc.tile_pool(name="work", bufs=2) as work,
         tc.psum_pool(name="psum", bufs=2) as psum,
+        tc.psum_pool(name="psum_per_chunk", bufs=CHUNKS) as psum_per_chunk,
     ):
         offsets = held.tile([P, EDGES // 16], U16, name="offsets")
         nc.sync.dma_start(offsets[:], offs)
 
-        tables = [held.tile([P, NODES], F32, name=f"table{b}") for b in range(BLOCKS)]
-        for b in range(BLOCKS):
-            nc.sync.dma_start(tables[b][:], x[b * P : (b + 1) * P, :])
-
+        tables = [held.tile([P, NODES], F32, name=f"table{b}") for b in range(4)]
+        for b in (1, 2, 3, 0):
+            nc.scalar.dma_start(tables[b][:], x[b * P : (b + 1) * P, :])
         norm_weights = held.tile([P, P], BF16, name="norm_weights")
         gate_weights = held.tile([P, P], BF16, name="gate_weights")
         scalar_bias = held.tile([P, 1], F32, name="scalar_bias")
         gate_bias = held.tile([P, 1], F32, name="gate_bias")
-        nc.sync.dma_start(norm_weights[:], w_norm)
-        nc.sync.dma_start(gate_weights[:], w_gate)
-        nc.sync.dma_start(scalar_bias[:], b_scalar)
-        nc.sync.dma_start(gate_bias[:], b_gate)
+        nc.scalar.dma_start(norm_weights[:], w_norm)
+        nc.scalar.dma_start(gate_weights[:], w_gate)
+        nc.scalar.dma_start(scalar_bias[:], b_scalar)
+        nc.scalar.dma_start(gate_bias[:], b_gate)
 
         identity = held.tile([P, P], F32, name="identity")
         make_identity(nc, identity[:])
         eps = held.tile([P, 1], F32, name="eps")
         nc.gpsimd.memset(eps[:], EPS)
 
-        for c in range(EDGES // CHUNK):
-            edges = slice(c * CHUNK, (c + 1) * CHUNK)
+        def look_up_and_add(b, c):
+            term = per_chunk.tile([P, CHUNK], F32, name=f"term{b}")
+            nc.sync.dma_start(term[:], other[b * P : (b + 1) * P, c * CHUNK : (c + 1) * CHUNK])
+            a = per_chunk.tile([P, CHUNK], F32, name=f"a{b}")
             piece = offsets[:, c * CHUNK // 16 : (c + 1) * CHUNK // 16]
+            nc.vector.tensor_tensor(a[:], tables[b][:].indirect(piece), term[:], ADD)
+            return a
 
-            summed = []
-            for b in range(BLOCKS):
-                term = work.tile([P, CHUNK], F32, name=f"term{b}")
-                nc.sync.dma_start(term[:], other[b * P : (b + 1) * P, edges])
-                a = work.tile([P, CHUNK], F32, name=f"a{b}")
-                nc.vector.tensor_tensor(a[:], tables[b][:].indirect(piece), term[:], ADD)
-                summed.append(a)
-            sp, vh = summed[0], summed[1:]
+        for first in range(0, CHUNKS, GROUP):
+            group = range(first, first + GROUP)
+            vh = {}
+            s_psum = {}
 
-            norm2 = psum.tile([P, CHUNK], F32, name="norm2")
-            for r in range(3):
-                squared = work.tile([P, CHUNK], F32, name=f"squared{r}")
-                nc.scalar.activation(squared[:], vh[r][:], ACT.Square)
-                nc.tensor.matmul(norm2[:], identity[:], squared[:], start=(r == 0), stop=(r == 2))
-            vn = work.tile([P, CHUNK], BF16, name="vn")
-            nc.scalar.activation(vn[:], norm2[:], ACT.Sqrt, bias=eps[:])
+            for c in group:
+                vh[c] = [look_up_and_add(1 + r, c) for r in range(3)]
+                norm2 = psum.tile([P, CHUNK], F32, name="norm2")
+                for r in range(3):
+                    squared = work.tile([P, CHUNK], F32, name=f"squared{r}")
+                    nc.scalar.activation(squared[:], vh[c][r][:], ACT.Square)
+                    nc.tensor.matmul(norm2[:], identity[:], squared[:], start=(r == 0), stop=(r == 2))
+                vn = work.tile([P, CHUNK], BF16, name="vn")
+                nc.scalar.activation(vn[:], norm2[:], ACT.Sqrt, bias=eps[:])
+                s_psum[c] = psum_per_chunk.tile([P, CHUNK], F32, name="s_psum")
+                nc.tensor.matmul(s_psum[c][:], norm_weights[:], vn[:], start=True, stop=False)
 
-            s_psum = psum.tile([P, CHUNK], F32, name="s_psum")
-            nc.tensor.matmul(s_psum[:], norm_weights[:], vn[:], start=True, stop=False)
-            nc.tensor.matmul(s_psum[:], identity[:], sp[:], start=False, stop=True)
-            s_bf16 = work.tile([P, CHUNK], BF16, name="s_bf16")
-            nc.scalar.activation(s_bf16[:], s_psum[:], ACT.Identity, bias=scalar_bias[:])
-            s_relu = work.tile([P, CHUNK], F32, name="s_relu")
-            nc.scalar.activation(s_relu[:], s_psum[:], ACT.Relu, bias=scalar_bias[:])
-            nc.sync.dma_start(out[0:P, edges], s_relu[:])
-
-            gate_psum = psum.tile([P, CHUNK], F32, name="gate_psum")
-            nc.tensor.matmul(gate_psum[:], gate_weights[:], s_bf16[:], start=True, stop=True)
-            gate = work.tile([P, CHUNK], F32, name="gate")
-            nc.scalar.activation(gate[:], gate_psum[:], ACT.Sigmoid, bias=gate_bias[:])
-
-            for r in range(3):
-                gated = work.tile([P, CHUNK], F32, name=f"gated{r}")
-                nc.gpsimd.tensor_tensor(gated[:], vh[r][:], gate[:], MULT)
-                nc.sync.dma_start(out[(1 + r) * P : (2 + r) * P, edges], gated[:])
+            for c in group:
+                edges = slice(c * CHUNK, (c + 1) * CHUNK)
+                sp = look_up_and_add(0, c)
+                nc.tensor.matmul(s_psum[c][:], identity[:], sp[:], start=False, stop=True)
+                s_bf16 = work.tile([P, CHUNK], BF16, name="s_bf16")
+                nc.scalar.activation(s_bf16[:], s_psum[c][:], ACT.Identity, bias=scalar_bias[:])
+                gate_psum = psum.tile([P, CHUNK], F32, name="gate_psum")
+                nc.tensor.matmul(gate_psum[:], gate_weights[:], s_bf16[:], start=True, stop=True)
+                gate = work.tile([P, CHUNK], F32, name="gate")
+                nc.scalar.activation(gate[:], gate_psum[:], ACT.Sigmoid, bias=gate_bias[:])
+                for r in range(3):
+                    gated = work.tile([P, CHUNK], F32, name=f"gated{r}")
+                    nc.gpsimd.tensor_tensor(gated[:], vh[c][r][:], gate[:], MULT)
+                    nc.sync.dma_start(out[(1 + r) * P : (2 + r) * P, edges], gated[:])
+                s_relu = work.tile([P, CHUNK], F32, name="s_relu")
+                nc.scalar.activation(s_relu[:], s_psum[c][:], ACT.Relu, bias=scalar_bias[:])
+                nc.sync.dma_start(out[0:P, edges], s_relu[:])

@@ -2,7 +2,7 @@ import concourse.mybir as mybir
 from concourse.masks import make_identity
 
 F32, BF16, U16 = mybir.dt.float32, mybir.dt.bfloat16, mybir.dt.uint16
-ADD, MULT = mybir.AluOpType.add, mybir.AluOpType.mult
+ADD, MULT, MAX = mybir.AluOpType.add, mybir.AluOpType.mult, mybir.AluOpType.max
 ACT = mybir.ActivationFunctionType
 
 P = 128
@@ -21,31 +21,35 @@ def tile_messagefunction_kernel(tc, x, other, w_norm, b_scalar, w_gate, b_gate, 
     with (
         tc.tile_pool(name="held", bufs=1) as held,
         tc.tile_pool(name="per_chunk", bufs=CHUNKS) as per_chunk,
-        tc.tile_pool(name="work", bufs=2) as work,
-        tc.psum_pool(name="psum", bufs=2) as psum,
+        tc.tile_pool(name="work", bufs=3) as work,
+        tc.psum_pool(name="psum", bufs=GROUP) as psum,
         tc.psum_pool(name="psum_per_chunk", bufs=CHUNKS) as psum_per_chunk,
     ):
         offsets = held.tile([P, EDGES // 16], U16, name="offsets")
         nc.sync.dma_start(offsets[:], offs)
 
-        tables = [held.tile([P, NODES], F32, name=f"table{b}") for b in range(4)]
-        for b in (1, 2, 3, 0):
-            nc.scalar.dma_start(tables[b][:], x[b * P : (b + 1) * P, :])
-        norm_weights = held.tile([P, P], BF16, name="norm_weights")
-        gate_weights = held.tile([P, P], BF16, name="gate_weights")
-        scalar_bias = held.tile([P, 1], F32, name="scalar_bias")
-        gate_bias = held.tile([P, 1], F32, name="gate_bias")
-        nc.scalar.dma_start(norm_weights[:], w_norm)
-        nc.scalar.dma_start(gate_weights[:], w_gate)
-        nc.scalar.dma_start(scalar_bias[:], b_scalar)
-        nc.scalar.dma_start(gate_bias[:], b_gate)
-
         identity = held.tile([P, P], F32, name="identity")
         make_identity(nc, identity[:])
         eps = held.tile([P, 1], F32, name="eps")
         nc.gpsimd.memset(eps[:], EPS)
+        table_set_warmer = held.tile([P, 1], F32, name="table_set_warmer")
+        nc.scalar.activation(table_set_warmer[:], eps[:], ACT.Sqrt)
+
+        norm_weights = held.tile([P, P], BF16, name="norm_weights")
+        gate_weights = held.tile([P, P], BF16, name="gate_weights")
+        scalar_bias = held.tile([P, 1], F32, name="scalar_bias")
+        gate_bias = held.tile([P, 1], F32, name="gate_bias")
+        nc.sync.dma_start(norm_weights[:], w_norm)
+        nc.sync.dma_start(scalar_bias[:], b_scalar)
+        nc.sync.dma_start(gate_weights[:], w_gate)
+        nc.sync.dma_start(gate_bias[:], b_gate)
+
+        tables = {}
 
         def look_up_and_add(b, c):
+            if b not in tables:
+                tables[b] = held.tile([P, NODES], F32, name=f"table{b}")
+                nc.sync.dma_start(tables[b][:], x[b * P : (b + 1) * P, :])
             term = per_chunk.tile([P, CHUNK], F32, name=f"term{b}")
             nc.sync.dma_start(term[:], other[b * P : (b + 1) * P, c * CHUNK : (c + 1) * CHUNK])
             a = per_chunk.tile([P, CHUNK], F32, name=f"a{b}")
@@ -53,37 +57,47 @@ def tile_messagefunction_kernel(tc, x, other, w_norm, b_scalar, w_gate, b_gate, 
             nc.vector.tensor_tensor(a[:], tables[b][:].indirect(piece), term[:], ADD)
             return a
 
+        vh, norm2, s_psum, gate_psum = {}, {}, {}, {}
         for first in range(0, CHUNKS, GROUP):
             group = range(first, first + GROUP)
-            vh = {}
-            s_psum = {}
+            vector_is_free = first + GROUP == CHUNKS
 
             for c in group:
                 vh[c] = [look_up_and_add(1 + r, c) for r in range(3)]
-                norm2 = psum.tile([P, CHUNK], F32, name="norm2")
+                norm2[c] = psum.tile([P, CHUNK], F32, name="norm2")
                 for r in range(3):
                     squared = work.tile([P, CHUNK], F32, name=f"squared{r}")
                     nc.scalar.activation(squared[:], vh[c][r][:], ACT.Square)
-                    nc.tensor.matmul(norm2[:], identity[:], squared[:], start=(r == 0), stop=(r == 2))
+                    nc.tensor.matmul(norm2[c][:], identity[:], squared[:], start=(r == 0), stop=(r == 2))
+
+            for c in group:
                 vn = work.tile([P, CHUNK], BF16, name="vn")
-                nc.scalar.activation(vn[:], norm2[:], ACT.Sqrt, bias=eps[:])
+                nc.scalar.activation(vn[:], norm2[c][:], ACT.Sqrt, bias=eps[:])
                 s_psum[c] = psum_per_chunk.tile([P, CHUNK], F32, name="s_psum")
                 nc.tensor.matmul(s_psum[c][:], norm_weights[:], vn[:], start=True, stop=False)
 
             for c in group:
-                edges = slice(c * CHUNK, (c + 1) * CHUNK)
                 sp = look_up_and_add(0, c)
                 nc.tensor.matmul(s_psum[c][:], identity[:], sp[:], start=False, stop=True)
+
+            for c in group:
                 s_bf16 = work.tile([P, CHUNK], BF16, name="s_bf16")
-                nc.scalar.activation(s_bf16[:], s_psum[c][:], ACT.Identity, bias=scalar_bias[:])
-                gate_psum = psum.tile([P, CHUNK], F32, name="gate_psum")
-                nc.tensor.matmul(gate_psum[:], gate_weights[:], s_bf16[:], start=True, stop=True)
+                if vector_is_free:
+                    nc.vector.tensor_scalar_add(s_bf16[:], s_psum[c][:], scalar_bias[:])
+                else:
+                    nc.scalar.activation(s_bf16[:], s_psum[c][:], ACT.Identity, bias=scalar_bias[:])
+                gate_psum[c] = psum.tile([P, CHUNK], F32, name="gate_psum")
+                nc.tensor.matmul(gate_psum[c][:], gate_weights[:], s_bf16[:], start=True, stop=True)
+
+            for c in group:
                 gate = work.tile([P, CHUNK], F32, name="gate")
-                nc.scalar.activation(gate[:], gate_psum[:], ACT.Sigmoid, bias=gate_bias[:])
+                nc.scalar.activation(gate[:], gate_psum[c][:], ACT.Sigmoid, bias=gate_bias[:])
                 for r in range(3):
                     gated = work.tile([P, CHUNK], F32, name=f"gated{r}")
-                    nc.gpsimd.tensor_tensor(gated[:], vh[c][r][:], gate[:], MULT)
-                    nc.sync.dma_start(out[(1 + r) * P : (2 + r) * P, edges], gated[:])
-                s_relu = work.tile([P, CHUNK], F32, name="s_relu")
-                nc.scalar.activation(s_relu[:], s_psum[c][:], ACT.Relu, bias=scalar_bias[:])
-                nc.sync.dma_start(out[0:P, edges], s_relu[:])
+                    nc.vector.tensor_tensor(gated[:], vh[c][r][:], gate[:], MULT)
+                    nc.sync.dma_start(out[(1 + r) * P : (2 + r) * P, c * CHUNK : (c + 1) * CHUNK], gated[:])
+
+        for c in range(CHUNKS):
+            s_relu = work.tile([P, CHUNK], F32, name="s_relu")
+            nc.vector.tensor_scalar(s_relu[:], s_psum[c][:], scalar_bias[:], 0.0, ADD, MAX)
+            nc.sync.dma_start(out[0:P, c * CHUNK : (c + 1) * CHUNK], s_relu[:])

@@ -94,7 +94,8 @@ def tile_messagefunction_kernel(tc, x, other, w_norm, b_scalar, w_gate, b_gate, 
                 nc.scalar.activation(gate[:], gate_psum[c][:], ACT.Sigmoid, bias=gate_bias[:])
                 for r in range(3):
                     gated = work.tile([P, CHUNK], F32, name=f"gated{r}")
-                    nc.vector.tensor_tensor(gated[:], vh[c][r][:], gate[:], MULT)
+                    engine = nc.vector if vector_is_free and r < 2 else nc.gpsimd
+                    engine.tensor_tensor(gated[:], vh[c][r][:], gate[:], MULT)
                     nc.sync.dma_start(out[(1 + r) * P : (2 + r) * P, c * CHUNK : (c + 1) * CHUNK], gated[:])
 
         for c in range(CHUNKS):

@@ -39,10 +39,6 @@ def tile_messagefunction_kernel(tc, x, other, w_norm, b_scalar, w_gate, b_gate, 
         gate_weights = held.tile([P, P], BF16, name="gate_weights")
         scalar_bias = held.tile([P, 1], F32, name="scalar_bias")
         gate_bias = held.tile([P, 1], F32, name="gate_bias")
-        nc.sync.dma_start(norm_weights[:], w_norm)
-        nc.sync.dma_start(scalar_bias[:], b_scalar)
-        nc.sync.dma_start(gate_weights[:], w_gate)
-        nc.sync.dma_start(gate_bias[:], b_gate)
 
         tables = {}
 
@@ -57,13 +53,18 @@ def tile_messagefunction_kernel(tc, x, other, w_norm, b_scalar, w_gate, b_gate, 
             nc.vector.tensor_tensor(a[:], tables[b][:].indirect(piece), term[:], ADD)
             return a
 
-        vh, norm2, s_psum, gate_psum = {}, {}, {}, {}
+        vh, norm2, s_psum, gate_psum, gate = {}, {}, {}, {}, {}
         for first in range(0, CHUNKS, GROUP):
             group = range(first, first + GROUP)
             vector_is_free = first + GROUP == CHUNKS
 
             for c in group:
                 vh[c] = [look_up_and_add(1 + r, c) for r in range(3)]
+                if c == 0:
+                    nc.sync.dma_start(norm_weights[:], w_norm)
+                    nc.sync.dma_start(scalar_bias[:], b_scalar)
+                    nc.sync.dma_start(gate_weights[:], w_gate)
+                    nc.sync.dma_start(gate_bias[:], b_gate)
                 norm2[c] = psum.tile([P, CHUNK], F32, name="norm2")
                 for r in range(3):
                     squared = work.tile([P, CHUNK], F32, name=f"squared{r}")
@@ -90,15 +91,19 @@ def tile_messagefunction_kernel(tc, x, other, w_norm, b_scalar, w_gate, b_gate, 
                 nc.tensor.matmul(gate_psum[c][:], gate_weights[:], s_bf16[:], start=True, stop=True)
 
             for c in group:
-                gate = work.tile([P, CHUNK], F32, name="gate")
-                nc.scalar.activation(gate[:], gate_psum[c][:], ACT.Sigmoid, bias=gate_bias[:])
-                for r in range(3):
-                    gated = work.tile([P, CHUNK], F32, name=f"gated{r}")
-                    engine = nc.vector if vector_is_free and r < 2 else nc.gpsimd
-                    engine.tensor_tensor(gated[:], vh[c][r][:], gate[:], MULT)
-                    nc.sync.dma_start(out[(1 + r) * P : (2 + r) * P, c * CHUNK : (c + 1) * CHUNK], gated[:])
+                gate[c] = per_chunk.tile([P, CHUNK], F32, name="gate")
+                nc.scalar.activation(gate[c][:], gate_psum[c][:], ACT.Sigmoid, bias=gate_bias[:])
+
+        for c in range(CHUNKS):
+            for r in range(3):
+                gated = work.tile([P, CHUNK], F32, name=f"gated{r}")
+                nc.vector.tensor_tensor(gated[:], vh[c][r][:], gate[c][:], MULT)
+                nc.sync.dma_start(out[(1 + r) * P : (2 + r) * P, c * CHUNK : (c + 1) * CHUNK], gated[:])
 
         for c in range(CHUNKS):
             s_relu = work.tile([P, CHUNK], F32, name="s_relu")
-            nc.vector.tensor_scalar(s_relu[:], s_psum[c][:], scalar_bias[:], 0.0, ADD, MAX)
+            if c < GROUP:
+                nc.scalar.activation(s_relu[:], s_psum[c][:], ACT.Relu, bias=scalar_bias[:])
+            else:
+                nc.vector.tensor_scalar(s_relu[:], s_psum[c][:], scalar_bias[:], 0.0, ADD, MAX)
             nc.sync.dma_start(out[0:P, c * CHUNK : (c + 1) * CHUNK], s_relu[:])

@@ -10,7 +10,6 @@ NODES = 512
 EDGES = 2048
 CHUNK = 512
 CHUNKS = EDGES // CHUNK
-GROUP = 2
 EPS = 1e-8
 
 FLOPS = 2 * 2 * P * P * EDGES
@@ -22,7 +21,7 @@ def tile_messagefunction_kernel(tc, x, other, w_norm, b_scalar, w_gate, b_gate, 
         tc.tile_pool(name="held", bufs=1) as held,
         tc.tile_pool(name="per_chunk", bufs=CHUNKS) as per_chunk,
         tc.tile_pool(name="work", bufs=3) as work,
-        tc.psum_pool(name="psum", bufs=GROUP) as psum,
+        tc.psum_pool(name="psum", bufs=2) as psum,
         tc.psum_pool(name="psum_per_chunk", bufs=CHUNKS) as psum_per_chunk,
     ):
         offsets = held.tile([P, EDGES // 16], U16, name="offsets")
@@ -32,15 +31,11 @@ def tile_messagefunction_kernel(tc, x, other, w_norm, b_scalar, w_gate, b_gate, 
         make_identity(nc, identity[:])
         eps = held.tile([P, 1], F32, name="eps")
         nc.gpsimd.memset(eps[:], EPS)
-        table_set_warmer = held.tile([P, 1], F32, name="table_set_warmer")
-        nc.scalar.activation(table_set_warmer[:], eps[:], ACT.Sqrt)
-
-        norm_weights = held.tile([P, P], BF16, name="norm_weights")
-        gate_weights = held.tile([P, P], BF16, name="gate_weights")
-        scalar_bias = held.tile([P, 1], F32, name="scalar_bias")
-        gate_bias = held.tile([P, 1], F32, name="gate_bias")
+        sqrt_set_warmer = held.tile([P, 1], F32, name="sqrt_set_warmer")
+        nc.scalar.activation(sqrt_set_warmer[:], eps[:], ACT.Sqrt)
 
         tables = {}
+        vh, norm2, vn, s_psum, sp, gate = {}, {}, {}, {}, {}, {}
 
         def look_up_and_add(b, c):
             if b not in tables:
@@ -53,57 +48,53 @@ def tile_messagefunction_kernel(tc, x, other, w_norm, b_scalar, w_gate, b_gate, 
             nc.vector.tensor_tensor(a[:], tables[b][:].indirect(piece), term[:], ADD)
             return a
 
-        vh, norm2, s_psum, gate_psum, gate = {}, {}, {}, {}, {}
-        for first in range(0, CHUNKS, GROUP):
-            group = range(first, first + GROUP)
-            vector_is_free = first + GROUP == CHUNKS
+        def squared_norm(c):
+            vh[c] = []
+            norm2[c] = psum.tile([P, CHUNK], F32, name="norm2")
+            for r in range(3):
+                vh[c].append(look_up_and_add(1 + r, c))
+                squared = work.tile([P, CHUNK], F32, name=f"squared{r}")
+                nc.scalar.activation(squared[:], vh[c][r][:], ACT.Square)
+                nc.tensor.matmul(norm2[c][:], identity[:], squared[:], start=(r == 0), stop=(r == 2))
 
-            for c in group:
-                vh[c] = [look_up_and_add(1 + r, c) for r in range(3)]
-                if c == 0:
-                    nc.sync.dma_start(norm_weights[:], w_norm)
-                    nc.sync.dma_start(scalar_bias[:], b_scalar)
-                    nc.sync.dma_start(gate_weights[:], w_gate)
-                    nc.sync.dma_start(gate_bias[:], b_gate)
-                norm2[c] = psum.tile([P, CHUNK], F32, name="norm2")
-                for r in range(3):
-                    squared = work.tile([P, CHUNK], F32, name=f"squared{r}")
-                    nc.scalar.activation(squared[:], vh[c][r][:], ACT.Square)
-                    nc.tensor.matmul(norm2[c][:], identity[:], squared[:], start=(r == 0), stop=(r == 2))
+        def norm_into_s(c):
+            vn[c] = work.tile([P, CHUNK], BF16, name="vn")
+            nc.scalar.activation(vn[c][:], norm2[c][:], ACT.Sqrt, bias=eps[:])
+            s_psum[c] = psum_per_chunk.tile([P, CHUNK], F32, name="s_psum")
+            nc.tensor.matmul(s_psum[c][:], norm_weights[:], vn[c][:], start=True, stop=False)
 
-            for c in group:
-                vn = work.tile([P, CHUNK], BF16, name="vn")
-                nc.scalar.activation(vn[:], norm2[c][:], ACT.Sqrt, bias=eps[:])
-                s_psum[c] = psum_per_chunk.tile([P, CHUNK], F32, name="s_psum")
-                nc.tensor.matmul(s_psum[c][:], norm_weights[:], vn[:], start=True, stop=False)
-
-            for c in group:
-                sp = look_up_and_add(0, c)
-                nc.tensor.matmul(s_psum[c][:], identity[:], sp[:], start=False, stop=True)
-
-            for c in group:
-                s_bf16 = work.tile([P, CHUNK], BF16, name="s_bf16")
-                if vector_is_free:
-                    nc.vector.tensor_scalar_add(s_bf16[:], s_psum[c][:], scalar_bias[:])
-                else:
-                    nc.scalar.activation(s_bf16[:], s_psum[c][:], ACT.Identity, bias=scalar_bias[:])
-                gate_psum[c] = psum.tile([P, CHUNK], F32, name="gate_psum")
-                nc.tensor.matmul(gate_psum[c][:], gate_weights[:], s_bf16[:], start=True, stop=True)
-
-            for c in group:
-                gate[c] = per_chunk.tile([P, CHUNK], F32, name="gate")
-                nc.scalar.activation(gate[c][:], gate_psum[c][:], ACT.Sigmoid, bias=gate_bias[:])
+        squared_norm(0)
+        norm_weights = held.tile([P, P], BF16, name="norm_weights")
+        gate_weights = held.tile([P, P], BF16, name="gate_weights")
+        scalar_bias = held.tile([P, 1], F32, name="scalar_bias")
+        gate_bias = held.tile([P, 1], F32, name="gate_bias")
+        nc.sync.dma_start(norm_weights[:], w_norm)
+        nc.sync.dma_start(scalar_bias[:], b_scalar)
+        nc.sync.dma_start(gate_weights[:], w_gate)
+        nc.sync.dma_start(gate_bias[:], b_gate)
+        for c in range(1, CHUNKS):
+            squared_norm(c)
+            norm_into_s(c - 1)
+        norm_into_s(CHUNKS - 1)
+        sigmoid_set_warmer = held.tile([P, 1], F32, name="sigmoid_set_warmer")
+        nc.scalar.activation(sigmoid_set_warmer[:], vn[CHUNKS - 1][:, 0:1], ACT.Sigmoid)
 
         for c in range(CHUNKS):
+            sp[c] = look_up_and_add(0, c)
+        for c in range(CHUNKS):
+            nc.tensor.matmul(s_psum[c][:], identity[:], sp[c][:], start=False, stop=True)
+            s_bf16 = work.tile([P, CHUNK], BF16, name="s_bf16")
+            nc.scalar.activation(s_bf16[:], s_psum[c][:], ACT.Identity, bias=scalar_bias[:])
+            gate_psum = psum.tile([P, CHUNK], F32, name="gate_psum")
+            nc.tensor.matmul(gate_psum[:], gate_weights[:], s_bf16[:], start=True, stop=True)
+            gate[c] = per_chunk.tile([P, CHUNK], F32, name="gate")
+            nc.scalar.activation(gate[c][:], gate_psum[:], ACT.Sigmoid, bias=gate_bias[:])
+        for c in range(CHUNKS):
+            edges = slice(c * CHUNK, (c + 1) * CHUNK)
             for r in range(3):
                 gated = work.tile([P, CHUNK], F32, name=f"gated{r}")
                 nc.vector.tensor_tensor(gated[:], vh[c][r][:], gate[c][:], MULT)
-                nc.sync.dma_start(out[(1 + r) * P : (2 + r) * P, c * CHUNK : (c + 1) * CHUNK], gated[:])
-
-        for c in range(CHUNKS):
+                nc.sync.dma_start(out[(1 + r) * P : (2 + r) * P, edges], gated[:])
             s_relu = work.tile([P, CHUNK], F32, name="s_relu")
-            if c < GROUP:
-                nc.scalar.activation(s_relu[:], s_psum[c][:], ACT.Relu, bias=scalar_bias[:])
-            else:
-                nc.vector.tensor_scalar(s_relu[:], s_psum[c][:], scalar_bias[:], 0.0, ADD, MAX)
-            nc.sync.dma_start(out[0:P, c * CHUNK : (c + 1) * CHUNK], s_relu[:])
+            nc.vector.tensor_scalar(s_relu[:], s_psum[c][:], scalar_bias[:], 0.0, ADD, MAX)
+            nc.sync.dma_start(out[0:P, edges], s_relu[:])

@@ -10,6 +10,7 @@ NODES = 512
 EDGES = 2048
 CHUNK = 512
 CHUNKS = EDGES // CHUNK
+GROUP = 2
 EPS = 1e-8
 
 FLOPS = 2 * 2 * P * P * EDGES
@@ -21,7 +22,7 @@ def tile_messagefunction_kernel(tc, x, other, w_norm, b_scalar, w_gate, b_gate, 
         tc.tile_pool(name="held", bufs=1) as held,
         tc.tile_pool(name="per_chunk", bufs=CHUNKS) as per_chunk,
         tc.tile_pool(name="work", bufs=3) as work,
-        tc.psum_pool(name="psum", bufs=2) as psum,
+        tc.psum_pool(name="psum", bufs=GROUP) as psum,
         tc.psum_pool(name="psum_per_chunk", bufs=CHUNKS) as psum_per_chunk,
     ):
         offsets = held.tile([P, EDGES // 16], U16, name="offsets")
@@ -31,11 +32,15 @@ def tile_messagefunction_kernel(tc, x, other, w_norm, b_scalar, w_gate, b_gate, 
         make_identity(nc, identity[:])
         eps = held.tile([P, 1], F32, name="eps")
         nc.gpsimd.memset(eps[:], EPS)
-        sqrt_set_warmer = held.tile([P, 1], F32, name="sqrt_set_warmer")
-        nc.scalar.activation(sqrt_set_warmer[:], eps[:], ACT.Sqrt)
+        table_set_warmer = held.tile([P, 1], F32, name="table_set_warmer")
+        nc.scalar.activation(table_set_warmer[:], eps[:], ACT.Sqrt)
+
+        norm_weights = held.tile([P, P], BF16, name="norm_weights")
+        gate_weights = held.tile([P, P], BF16, name="gate_weights")
+        scalar_bias = held.tile([P, 1], F32, name="scalar_bias")
+        gate_bias = held.tile([P, 1], F32, name="gate_bias")
 
         tables = {}
-        vh, norm2, vn, s_psum, sp, gate = {}, {}, {}, {}, {}, {}
 
         def look_up_and_add(b, c):
             if b not in tables:
@@ -48,53 +53,61 @@ def tile_messagefunction_kernel(tc, x, other, w_norm, b_scalar, w_gate, b_gate, 
             nc.vector.tensor_tensor(a[:], tables[b][:].indirect(piece), term[:], ADD)
             return a
 
-        def squared_norm(c):
-            vh[c] = []
-            norm2[c] = psum.tile([P, CHUNK], F32, name="norm2")
-            for r in range(3):
-                vh[c].append(look_up_and_add(1 + r, c))
-                squared = work.tile([P, CHUNK], F32, name=f"squared{r}")
-                nc.scalar.activation(squared[:], vh[c][r][:], ACT.Square)
-                nc.tensor.matmul(norm2[c][:], identity[:], squared[:], start=(r == 0), stop=(r == 2))
+        vh, norm2, s_psum, sp, s_no_bias, gate_psum, gate = {}, {}, {}, {}, {}, {}, {}
+        for first in range(0, CHUNKS, GROUP):
+            group = range(first, first + GROUP)
+            vector_is_free = first + GROUP == CHUNKS
 
-        def norm_into_s(c):
-            vn[c] = work.tile([P, CHUNK], BF16, name="vn")
-            nc.scalar.activation(vn[c][:], norm2[c][:], ACT.Sqrt, bias=eps[:])
-            s_psum[c] = psum_per_chunk.tile([P, CHUNK], F32, name="s_psum")
-            nc.tensor.matmul(s_psum[c][:], norm_weights[:], vn[c][:], start=True, stop=False)
+            for c in group:
+                vh[c] = [look_up_and_add(1 + r, c) for r in range(3)]
+                if c == 0:
+                    nc.sync.dma_start(norm_weights[:], w_norm)
+                    nc.sync.dma_start(scalar_bias[:], b_scalar)
+                    nc.sync.dma_start(gate_weights[:], w_gate)
+                    nc.sync.dma_start(gate_bias[:], b_gate)
+                norm2[c] = psum.tile([P, CHUNK], F32, name="norm2")
+                for r in range(3):
+                    squared = work.tile([P, CHUNK], F32, name=f"squared{r}")
+                    nc.scalar.activation(squared[:], vh[c][r][:], ACT.Square)
+                    nc.tensor.matmul(norm2[c][:], identity[:], squared[:], start=(r == 0), stop=(r == 2))
 
-        squared_norm(0)
-        norm_weights = held.tile([P, P], BF16, name="norm_weights")
-        gate_weights = held.tile([P, P], BF16, name="gate_weights")
-        scalar_bias = held.tile([P, 1], F32, name="scalar_bias")
-        gate_bias = held.tile([P, 1], F32, name="gate_bias")
-        nc.sync.dma_start(norm_weights[:], w_norm)
-        nc.sync.dma_start(scalar_bias[:], b_scalar)
-        nc.sync.dma_start(gate_weights[:], w_gate)
-        nc.sync.dma_start(gate_bias[:], b_gate)
-        for c in range(1, CHUNKS):
-            squared_norm(c)
-            norm_into_s(c - 1)
-        norm_into_s(CHUNKS - 1)
-        sigmoid_set_warmer = held.tile([P, 1], F32, name="sigmoid_set_warmer")
-        nc.scalar.activation(sigmoid_set_warmer[:], vn[CHUNKS - 1][:, 0:1], ACT.Sigmoid)
+            for c in group:
+                vn = work.tile([P, CHUNK], BF16, name="vn")
+                nc.scalar.activation(vn[:], norm2[c][:], ACT.Sqrt, bias=eps[:])
+                s_psum[c] = psum_per_chunk.tile([P, CHUNK], F32, name="s_psum")
+                nc.tensor.matmul(s_psum[c][:], norm_weights[:], vn[:], start=True, stop=vector_is_free)
+
+            for c in group:
+                sp[c] = look_up_and_add(0, c)
+                if not vector_is_free:
+                    nc.tensor.matmul(s_psum[c][:], identity[:], sp[c][:], start=False, stop=True)
+                    s_no_bias[c] = s_psum[c]
+
+            for c in group:
+                s_bf16 = work.tile([P, CHUNK], BF16, name="s_bf16")
+                if vector_is_free:
+                    s_no_bias[c] = work.tile([P, CHUNK], F32, name="s_sum")
+                    nc.vector.tensor_tensor(s_no_bias[c][:], s_psum[c][:], sp[c][:], ADD)
+                    nc.vector.tensor_scalar_add(s_bf16[:], s_no_bias[c][:], scalar_bias[:])
+                else:
+                    nc.scalar.activation(s_bf16[:], s_psum[c][:], ACT.Identity, bias=scalar_bias[:])
+                gate_psum[c] = psum.tile([P, CHUNK], F32, name="gate_psum")
+                nc.tensor.matmul(gate_psum[c][:], gate_weights[:], s_bf16[:], start=True, stop=True)
+
+            for c in group:
+                gate[c] = per_chunk.tile([P, CHUNK], F32, name="gate")
+                nc.scalar.activation(gate[c][:], gate_psum[c][:], ACT.Sigmoid, bias=gate_bias[:])
 
         for c in range(CHUNKS):
-            sp[c] = look_up_and_add(0, c)
-        for c in range(CHUNKS):
-            nc.tensor.matmul(s_psum[c][:], identity[:], sp[c][:], start=False, stop=True)
-            s_bf16 = work.tile([P, CHUNK], BF16, name="s_bf16")
-            nc.scalar.activation(s_bf16[:], s_psum[c][:], ACT.Identity, bias=scalar_bias[:])
-            gate_psum = psum.tile([P, CHUNK], F32, name="gate_psum")
-            nc.tensor.matmul(gate_psum[:], gate_weights[:], s_bf16[:], start=True, stop=True)
-            gate[c] = per_chunk.tile([P, CHUNK], F32, name="gate")
-            nc.scalar.activation(gate[c][:], gate_psum[:], ACT.Sigmoid, bias=gate_bias[:])
-        for c in range(CHUNKS):
-            edges = slice(c * CHUNK, (c + 1) * CHUNK)
             for r in range(3):
                 gated = work.tile([P, CHUNK], F32, name=f"gated{r}")
                 nc.vector.tensor_tensor(gated[:], vh[c][r][:], gate[c][:], MULT)
-                nc.sync.dma_start(out[(1 + r) * P : (2 + r) * P, edges], gated[:])
+                nc.sync.dma_start(out[(1 + r) * P : (2 + r) * P, c * CHUNK : (c + 1) * CHUNK], gated[:])
+
+        for c in range(CHUNKS):
             s_relu = work.tile([P, CHUNK], F32, name="s_relu")
-            nc.vector.tensor_scalar(s_relu[:], s_psum[c][:], scalar_bias[:], 0.0, ADD, MAX)
-            nc.sync.dma_start(out[0:P, edges], s_relu[:])
+            if c < GROUP:
+                nc.scalar.activation(s_relu[:], s_no_bias[c][:], ACT.Relu, bias=scalar_bias[:])
+            else:
+                nc.vector.tensor_scalar(s_relu[:], s_no_bias[c][:], scalar_bias[:], 0.0, ADD, MAX)
+            nc.sync.dma_start(out[0:P, c * CHUNK : (c + 1) * CHUNK], s_relu[:])

@@ -8,10 +8,12 @@ ACT = mybir.ActivationFunctionType
 P = 128
 NODES = 512
 EDGES = 2048
-CHUNK = 512
-CHUNKS = EDGES // CHUNK
-GROUP = 2
+BANK = 512
 EPS = 1e-8
+
+FIRST_GROUP = [(0, BANK), (BANK, BANK)]
+LAST_GROUP = [(2 * BANK + i * BANK // 2, BANK // 2) for i in range(4)]
+PIECES = FIRST_GROUP + LAST_GROUP
 
 FLOPS = 2 * 2 * P * P * EDGES
 
@@ -20,10 +22,8 @@ def tile_messagefunction_kernel(tc, x, other, w_norm, b_scalar, w_gate, b_gate, 
     nc = tc.nc
     with (
         tc.tile_pool(name="held", bufs=1) as held,
-        tc.tile_pool(name="per_chunk", bufs=CHUNKS) as per_chunk,
         tc.tile_pool(name="work", bufs=3) as work,
-        tc.psum_pool(name="psum", bufs=GROUP) as psum,
-        tc.psum_pool(name="psum_per_chunk", bufs=CHUNKS) as psum_per_chunk,
+        tc.psum_pool(name="psum", bufs=4) as psum,
     ):
         offsets = held.tile([P, EDGES // 16], U16, name="offsets")
         nc.sync.dma_start(offsets[:], offs)
@@ -42,72 +42,77 @@ def tile_messagefunction_kernel(tc, x, other, w_norm, b_scalar, w_gate, b_gate, 
 
         tables = {}
 
-        def look_up_and_add(b, c):
+        def look_up_and_add(b, piece):
+            first, width = piece
             if b not in tables:
                 tables[b] = held.tile([P, NODES], F32, name=f"table{b}")
                 nc.sync.dma_start(tables[b][:], x[b * P : (b + 1) * P, :])
-            term = per_chunk.tile([P, CHUNK], F32, name=f"term{b}")
-            nc.sync.dma_start(term[:], other[b * P : (b + 1) * P, c * CHUNK : (c + 1) * CHUNK])
-            a = per_chunk.tile([P, CHUNK], F32, name=f"a{b}")
-            piece = offsets[:, c * CHUNK // 16 : (c + 1) * CHUNK // 16]
-            nc.vector.tensor_tensor(a[:], tables[b][:].indirect(piece), term[:], ADD)
+            term = held.tile([P, width], F32, name=f"term{b}_{first}")
+            nc.sync.dma_start(term[:], other[b * P : (b + 1) * P, first : first + width])
+            a = held.tile([P, width], F32, name=f"a{b}_{first}")
+            nc.vector.tensor_tensor(a[:], tables[b][:].indirect(offsets[:, first // 16 : (first + width) // 16]), term[:], ADD)
             return a
 
         vh, norm2, s_psum, sp, s_no_bias, gate_psum, gate = {}, {}, {}, {}, {}, {}, {}
-        for first in range(0, CHUNKS, GROUP):
-            group = range(first, first + GROUP)
-            vector_is_free = first + GROUP == CHUNKS
+        for group in (FIRST_GROUP, LAST_GROUP):
+            vector_is_free = group is LAST_GROUP
 
-            for c in group:
-                vh[c] = [look_up_and_add(1 + r, c) for r in range(3)]
-                if c == 0:
+            for piece in group:
+                first, width = piece
+                vh[piece] = [look_up_and_add(1 + r, piece) for r in range(3)]
+                if first == 0:
                     nc.sync.dma_start(norm_weights[:], w_norm)
                     nc.sync.dma_start(scalar_bias[:], b_scalar)
                     nc.sync.dma_start(gate_weights[:], w_gate)
                     nc.sync.dma_start(gate_bias[:], b_gate)
-                norm2[c] = psum.tile([P, CHUNK], F32, name="norm2")
+                norm2[piece] = psum.tile([P, width], F32, name="norm2", tag="read_once")
                 for r in range(3):
-                    squared = work.tile([P, CHUNK], F32, name=f"squared{r}")
-                    nc.scalar.activation(squared[:], vh[c][r][:], ACT.Square)
-                    nc.tensor.matmul(norm2[c][:], identity[:], squared[:], start=(r == 0), stop=(r == 2))
+                    squared = work.tile([P, width], F32, name=f"squared{r}_{width}")
+                    nc.scalar.activation(squared[:], vh[piece][r][:], ACT.Square)
+                    nc.tensor.matmul(norm2[piece][:], identity[:], squared[:], start=(r == 0), stop=(r == 2))
 
-            for c in group:
-                vn = work.tile([P, CHUNK], BF16, name="vn")
-                nc.scalar.activation(vn[:], norm2[c][:], ACT.Sqrt, bias=eps[:])
-                s_psum[c] = psum_per_chunk.tile([P, CHUNK], F32, name="s_psum")
-                nc.tensor.matmul(s_psum[c][:], norm_weights[:], vn[:], start=True, stop=vector_is_free)
+            for piece in group:
+                first, width = piece
+                vn = work.tile([P, width], BF16, name=f"vn_{width}")
+                nc.scalar.activation(vn[:], norm2[piece][:], ACT.Sqrt, bias=eps[:])
+                s_psum[piece] = psum.tile([P, width], F32, name="s_psum")
+                nc.tensor.matmul(s_psum[piece][:], norm_weights[:], vn[:], start=True, stop=vector_is_free)
 
-            for c in group:
-                sp[c] = look_up_and_add(0, c)
+            for piece in group:
+                sp[piece] = look_up_and_add(0, piece)
                 if not vector_is_free:
-                    nc.tensor.matmul(s_psum[c][:], identity[:], sp[c][:], start=False, stop=True)
-                    s_no_bias[c] = s_psum[c]
+                    nc.tensor.matmul(s_psum[piece][:], identity[:], sp[piece][:], start=False, stop=True)
+                    s_no_bias[piece] = s_psum[piece]
 
-            for c in group:
-                s_bf16 = work.tile([P, CHUNK], BF16, name="s_bf16")
+            for piece in group:
+                first, width = piece
+                s_bf16 = work.tile([P, width], BF16, name=f"s_bf16_{width}")
                 if vector_is_free:
-                    s_no_bias[c] = work.tile([P, CHUNK], F32, name="s_sum")
-                    nc.vector.tensor_tensor(s_no_bias[c][:], s_psum[c][:], sp[c][:], ADD)
-                    nc.vector.tensor_scalar_add(s_bf16[:], s_no_bias[c][:], scalar_bias[:])
+                    s_no_bias[piece] = held.tile([P, width], F32, name=f"s_sum{first}")
+                    nc.vector.tensor_tensor(s_no_bias[piece][:], s_psum[piece][:], sp[piece][:], ADD)
+                    nc.vector.tensor_scalar_add(s_bf16[:], s_no_bias[piece][:], scalar_bias[:])
                 else:
-                    nc.scalar.activation(s_bf16[:], s_psum[c][:], ACT.Identity, bias=scalar_bias[:])
-                gate_psum[c] = psum.tile([P, CHUNK], F32, name="gate_psum")
-                nc.tensor.matmul(gate_psum[c][:], gate_weights[:], s_bf16[:], start=True, stop=True)
+                    nc.scalar.activation(s_bf16[:], s_psum[piece][:], ACT.Identity, bias=scalar_bias[:])
+                gate_psum[piece] = psum.tile([P, width], F32, name="gate_psum", tag="read_once")
+                nc.tensor.matmul(gate_psum[piece][:], gate_weights[:], s_bf16[:], start=True, stop=True)
 
-            for c in group:
-                gate[c] = per_chunk.tile([P, CHUNK], F32, name="gate")
-                nc.scalar.activation(gate[c][:], gate_psum[c][:], ACT.Sigmoid, bias=gate_bias[:])
+            for piece in group:
+                first, width = piece
+                gate[piece] = held.tile([P, width], F32, name=f"gate{first}")
+                nc.scalar.activation(gate[piece][:], gate_psum[piece][:], ACT.Sigmoid, bias=gate_bias[:])
 
-        for c in range(CHUNKS):
+        for piece in PIECES:
+            first, width = piece
             for r in range(3):
-                gated = work.tile([P, CHUNK], F32, name=f"gated{r}")
-                nc.vector.tensor_tensor(gated[:], vh[c][r][:], gate[c][:], MULT)
-                nc.sync.dma_start(out[(1 + r) * P : (2 + r) * P, c * CHUNK : (c + 1) * CHUNK], gated[:])
+                gated = work.tile([P, width], F32, name=f"gated{r}_{width}")
+                nc.vector.tensor_tensor(gated[:], vh[piece][r][:], gate[piece][:], MULT)
+                nc.sync.dma_start(out[(1 + r) * P : (2 + r) * P, first : first + width], gated[:])
 
-        for c in range(CHUNKS):
-            s_relu = work.tile([P, CHUNK], F32, name="s_relu")
-            if c < GROUP:
-                nc.scalar.activation(s_relu[:], s_no_bias[c][:], ACT.Relu, bias=scalar_bias[:])
+        for piece in PIECES:
+            first, width = piece
+            s_relu = work.tile([P, width], F32, name=f"s_relu_{width}")
+            if piece in FIRST_GROUP:
+                nc.scalar.activation(s_relu[:], s_no_bias[piece][:], ACT.Relu, bias=scalar_bias[:])
             else:
-                nc.vector.tensor_scalar(s_relu[:], s_no_bias[c][:], scalar_bias[:], 0.0, ADD, MAX)
-            nc.sync.dma_start(out[0:P, c * CHUNK : (c + 1) * CHUNK], s_relu[:])
+                nc.vector.tensor_scalar(s_relu[:], s_no_bias[piece][:], scalar_bias[:], 0.0, ADD, MAX)
+            nc.sync.dma_start(out[0:P, first : first + width], s_relu[:])

@@ -42,16 +42,14 @@ def tile_messagefunction_kernel(tc, x, other, w_norm, b_scalar, w_gate, b_gate, 
 
         tables = {}
 
-        def look_up_and_add(b, piece):
+        def look_up_and_add(b, piece, a):
             first, width = piece
             if b not in tables:
                 tables[b] = held.tile([P, NODES], F32, name=f"table{b}")
                 nc.sync.dma_start(tables[b][:], x[b * P : (b + 1) * P, :])
             term = held.tile([P, width], F32, name=f"term{b}_{first}")
             nc.sync.dma_start(term[:], other[b * P : (b + 1) * P, first : first + width])
-            a = held.tile([P, width], F32, name=f"a{b}_{first}")
-            nc.vector.tensor_tensor(a[:], tables[b][:].indirect(offsets[:, first // 16 : (first + width) // 16]), term[:], ADD)
-            return a
+            nc.vector.tensor_tensor(a, tables[b][:].indirect(offsets[:, first // 16 : (first + width) // 16]), term[:], ADD)
 
         vh, norm2, s_psum, sp, s_no_bias, gate_psum, gate = {}, {}, {}, {}, {}, {}, {}
         for group in (FIRST_GROUP, LAST_GROUP):
@@ -59,7 +57,9 @@ def tile_messagefunction_kernel(tc, x, other, w_norm, b_scalar, w_gate, b_gate, 
 
             for piece in group:
                 first, width = piece
-                vh[piece] = [look_up_and_add(1 + r, piece) for r in range(3)]
+                vh[piece] = held.tile([P, 3, width], F32, name=f"vh{first}")
+                for r in range(3):
+                    look_up_and_add(1 + r, piece, vh[piece][:, r, :])
                 if first == 0:
                     nc.sync.dma_start(norm_weights[:], w_norm)
                     nc.sync.dma_start(scalar_bias[:], b_scalar)
@@ -68,7 +68,7 @@ def tile_messagefunction_kernel(tc, x, other, w_norm, b_scalar, w_gate, b_gate, 
                 norm2[piece] = psum.tile([P, width], F32, name="norm2", tag="read_once")
                 for r in range(3):
                     squared = work.tile([P, width], F32, name=f"squared{r}_{width}")
-                    nc.scalar.activation(squared[:], vh[piece][r][:], ACT.Square)
+                    nc.scalar.activation(squared[:], vh[piece][:, r, :], ACT.Square)
                     nc.tensor.matmul(norm2[piece][:], identity[:], squared[:], start=(r == 0), stop=(r == 2))
 
             for piece in group:
@@ -79,7 +79,8 @@ def tile_messagefunction_kernel(tc, x, other, w_norm, b_scalar, w_gate, b_gate, 
                 nc.tensor.matmul(s_psum[piece][:], norm_weights[:], vn[:], start=True, stop=vector_is_free)
 
             for piece in group:
-                sp[piece] = look_up_and_add(0, piece)
+                sp[piece] = held.tile([P, piece[1]], F32, name=f"sp{piece[0]}")
+                look_up_and_add(0, piece, sp[piece][:])
                 if not vector_is_free:
                     nc.tensor.matmul(s_psum[piece][:], identity[:], sp[piece][:], start=False, stop=True)
                     s_no_bias[piece] = s_psum[piece]
@@ -103,10 +104,15 @@ def tile_messagefunction_kernel(tc, x, other, w_norm, b_scalar, w_gate, b_gate, 
 
         for piece in PIECES:
             first, width = piece
-            for r in range(3):
-                gated = work.tile([P, width], F32, name=f"gated{r}_{width}")
-                nc.vector.tensor_tensor(gated[:], vh[piece][r][:], gate[piece][:], MULT)
-                nc.sync.dma_start(out[(1 + r) * P : (2 + r) * P, first : first + width], gated[:])
+            gated = work.tile([P, 3, width], F32, name=f"gated_{width}")
+            if piece is not PIECES[-1]:
+                gate_for_all = gate[piece][:].unsqueeze(1).to_broadcast([P, 3, width])
+                nc.vector.tensor_tensor(gated[:], vh[piece][:], gate_for_all, MULT)
+                nc.sync.dma_start(out[P : 4 * P, first : first + width].rearrange("(r p) j -> p r j", p=P), gated[:])
+            else:
+                for r in range(3):
+                    nc.vector.tensor_tensor(gated[:, r, :], vh[piece][:, r, :], gate[piece][:], MULT)
+                    nc.sync.dma_start(out[(1 + r) * P : (2 + r) * P, first : first + width], gated[:, r, :])
 
         for piece in PIECES:
             first, width = piece

@@ -105,20 +105,19 @@ def tile_messagefunction_kernel(tc, x, other, w_norm, b_scalar, w_gate, b_gate, 
         for piece in PIECES:
             first, width = piece
             gated = work.tile([P, 3, width], F32, name=f"gated_{width}")
-            if piece is not PIECES[-1]:
-                gate_for_all = gate[piece][:].unsqueeze(1).to_broadcast([P, 3, width])
-                nc.vector.tensor_tensor(gated[:], vh[piece][:], gate_for_all, MULT)
-                nc.sync.dma_start(out[P : 4 * P, first : first + width].rearrange("(r p) j -> p r j", p=P), gated[:])
-            else:
-                for r in range(3):
-                    nc.vector.tensor_tensor(gated[:, r, :], vh[piece][:, r, :], gate[piece][:], MULT)
-                    nc.sync.dma_start(out[(1 + r) * P : (2 + r) * P, first : first + width], gated[:, r, :])
+            gate_for_all = gate[piece][:].unsqueeze(1).to_broadcast([P, 3, width])
+            nc.vector.tensor_tensor(gated[:], vh[piece][:], gate_for_all, MULT)
+            nc.sync.dma_start(out[P : 4 * P, first : first + width].rearrange("(r p) j -> p r j", p=P), gated[:])
 
-        for piece in PIECES:
-            first, width = piece
-            s_relu = work.tile([P, width], F32, name=f"s_relu_{width}")
-            if piece in FIRST_GROUP:
-                nc.scalar.activation(s_relu[:], s_no_bias[piece][:], ACT.Relu, bias=scalar_bias[:])
-            else:
-                nc.vector.tensor_scalar(s_relu[:], s_no_bias[piece][:], scalar_bias[:], 0.0, ADD, MAX)
-            nc.sync.dma_start(out[0:P, first : first + width], s_relu[:])
+        for group in (FIRST_GROUP, LAST_GROUP):
+            group_first = group[0][0]
+            group_width = sum(width for first, width in group)
+            s_relu = held.tile([P, group_width], F32, name=f"s_relu{group_first}")
+            for piece in group:
+                first, width = piece
+                here = s_relu[:, first - group_first : first - group_first + width]
+                if group is FIRST_GROUP:
+                    nc.scalar.activation(here, s_no_bias[piece][:], ACT.Relu, bias=scalar_bias[:])
+                else:
+                    nc.vector.tensor_scalar(here, s_no_bias[piece][:], scalar_bias[:], 0.0, ADD, MAX)
+            nc.sync.dma_start(out[0:P, group_first : group_first + group_width], s_relu[:])

@@ -104,9 +104,9 @@ def tile_messagefunction_kernel(tc, x, other, w_norm, b_scalar, w_gate, b_gate, 
 
         for piece in PIECES:
             first, width = piece
-            gated = work.tile([P, 3, width], F32, name=f"gated_{width}")
-            gate_for_all = gate[piece][:].unsqueeze(1).to_broadcast([P, 3, width])
-            nc.vector.tensor_tensor(gated[:], vh[piece][:], gate_for_all, MULT)
+            gated = held.tile([P, 3, width], F32, name=f"gated{first}")
+            for r in range(3):
+                nc.vector.tensor_tensor(gated[:, r, :], vh[piece][:, r, :], gate[piece][:], MULT)
             nc.sync.dma_start(out[P : 4 * P, first : first + width].rearrange("(r p) j -> p r j", p=P), gated[:])
 
         for group in (FIRST_GROUP, LAST_GROUP):

@@ -13,6 +13,7 @@ EPS = 1e-8
 
 FIRST_GROUP = [(0, BANK), (BANK, BANK)]
 LAST_GROUP = [(2 * BANK + i * BANK // 2, BANK // 2) for i in range(4)]
+LAST_GROUP_WIDE = [(2 * BANK, BANK), (3 * BANK, BANK)]
 PIECES = FIRST_GROUP + LAST_GROUP
 
 FLOPS = 2 * 2 * P * P * EDGES
@@ -52,6 +53,7 @@ def tile_messagefunction_kernel(tc, x, other, w_norm, b_scalar, w_gate, b_gate, 
             nc.vector.tensor_tensor(a, tables[b][:].indirect(offsets[:, first // 16 : (first + width) // 16]), term[:], ADD)
 
         vh, norm2, s_psum, sp, s_no_bias, gate_psum, gate = {}, {}, {}, {}, {}, {}, {}
+        s_sum = held.tile([P, 2 * BANK], F32, name="s_sum")
         for group in (FIRST_GROUP, LAST_GROUP):
             vector_is_free = group is LAST_GROUP
 
@@ -78,20 +80,24 @@ def tile_messagefunction_kernel(tc, x, other, w_norm, b_scalar, w_gate, b_gate, 
                 s_psum[piece] = psum.tile([P, width], F32, name="s_psum")
                 nc.tensor.matmul(s_psum[piece][:], norm_weights[:], vn[:], start=True, stop=vector_is_free)
 
+            for wide in FIRST_GROUP if group is FIRST_GROUP else LAST_GROUP_WIDE:
+                sp_wide = held.tile([P, BANK], F32, name=f"sp{wide[0]}")
+                look_up_and_add(0, wide, sp_wide[:])
+                for piece in group:
+                    if wide[0] <= piece[0] < wide[0] + BANK:
+                        sp[piece] = sp_wide[:, piece[0] - wide[0] : piece[0] - wide[0] + piece[1]]
             for piece in group:
-                sp[piece] = held.tile([P, piece[1]], F32, name=f"sp{piece[0]}")
-                look_up_and_add(0, piece, sp[piece][:])
                 if not vector_is_free:
-                    nc.tensor.matmul(s_psum[piece][:], identity[:], sp[piece][:], start=False, stop=True)
-                    s_no_bias[piece] = s_psum[piece]
+                    nc.tensor.matmul(s_psum[piece][:], identity[:], sp[piece], start=False, stop=True)
+                    s_no_bias[piece] = s_psum[piece][:]
 
             for piece in group:
                 first, width = piece
                 s_bf16 = work.tile([P, width], BF16, name=f"s_bf16_{width}")
                 if vector_is_free:
-                    s_no_bias[piece] = held.tile([P, width], F32, name=f"s_sum{first}")
-                    nc.vector.tensor_tensor(s_no_bias[piece][:], s_psum[piece][:], sp[piece][:], ADD)
-                    nc.vector.tensor_scalar_add(s_bf16[:], s_no_bias[piece][:], scalar_bias[:])
+                    s_no_bias[piece] = s_sum[:, first - LAST_GROUP[0][0] : first - LAST_GROUP[0][0] + width]
+                    nc.vector.tensor_tensor(s_no_bias[piece], s_psum[piece][:], sp[piece], ADD)
+                    nc.vector.tensor_scalar_add(s_bf16[:], s_no_bias[piece], scalar_bias[:])
                 else:
                     nc.scalar.activation(s_bf16[:], s_psum[piece][:], ACT.Identity, bias=scalar_bias[:])
                 gate_psum[piece] = psum.tile([P, width], F32, name="gate_psum", tag="read_once")
@@ -105,19 +111,14 @@ def tile_messagefunction_kernel(tc, x, other, w_norm, b_scalar, w_gate, b_gate, 
         for piece in PIECES:
             first, width = piece
             gated = held.tile([P, 3, width], F32, name=f"gated{first}")
-            for r in range(3):
-                nc.vector.tensor_tensor(gated[:, r, :], vh[piece][:, r, :], gate[piece][:], MULT)
+            gate_for_all = gate[piece][:].unsqueeze(1).to_broadcast([P, 3, width])
+            nc.vector.tensor_tensor(gated[:], vh[piece][:], gate_for_all, MULT)
             nc.sync.dma_start(out[P : 4 * P, first : first + width].rearrange("(r p) j -> p r j", p=P), gated[:])
 
-        for group in (FIRST_GROUP, LAST_GROUP):
-            group_first = group[0][0]
-            group_width = sum(width for first, width in group)
-            s_relu = held.tile([P, group_width], F32, name=f"s_relu{group_first}")
-            for piece in group:
-                first, width = piece
-                here = s_relu[:, first - group_first : first - group_first + width]
-                if group is FIRST_GROUP:
-                    nc.scalar.activation(here, s_no_bias[piece][:], ACT.Relu, bias=scalar_bias[:])
-                else:
-                    nc.vector.tensor_scalar(here, s_no_bias[piece][:], scalar_bias[:], 0.0, ADD, MAX)
-            nc.sync.dma_start(out[0:P, group_first : group_first + group_width], s_relu[:])
+        s_relu_first = held.tile([P, 2 * BANK], F32, name="s_relu_first")
+        for first, width in FIRST_GROUP:
+            nc.scalar.activation(s_relu_first[:, first : first + width], s_no_bias[first, width], ACT.Relu, bias=scalar_bias[:])
+        nc.sync.dma_start(out[0:P, 0 : 2 * BANK], s_relu_first[:])
+        s_relu_last = held.tile([P, 2 * BANK], F32, name="s_relu_last")
+        nc.vector.tensor_scalar(s_relu_last[:], s_sum[:], scalar_bias[:], 0.0, ADD, MAX)
+        nc.sync.dma_start(out[0:P, 2 * BANK : EDGES], s_relu_last[:])

@@ -23,7 +23,6 @@ def tile_messagefunction_kernel(tc, x, other, w_norm, b_scalar, w_gate, b_gate, 
     nc = tc.nc
     with (
         tc.tile_pool(name="held", bufs=1) as held,
-        tc.tile_pool(name="work", bufs=3) as work,
         tc.psum_pool(name="psum", bufs=4) as psum,
     ):
         offsets = held.tile([P, EDGES // 16], U16, name="offsets")
@@ -69,13 +68,13 @@ def tile_messagefunction_kernel(tc, x, other, w_norm, b_scalar, w_gate, b_gate, 
                     nc.sync.dma_start(gate_bias[:], b_gate)
                 norm2[piece] = psum.tile([P, width], F32, name="norm2", tag="read_once")
                 for r in range(3):
-                    squared = work.tile([P, width], F32, name=f"squared{r}_{width}")
+                    squared = held.tile([P, width], F32, name=f"squared{r}_{first}")
                     nc.scalar.activation(squared[:], vh[piece][:, r, :], ACT.Square)
                     nc.tensor.matmul(norm2[piece][:], identity[:], squared[:], start=(r == 0), stop=(r == 2))
 
             for piece in group:
                 first, width = piece
-                vn = work.tile([P, width], BF16, name=f"vn_{width}")
+                vn = held.tile([P, width], BF16, name=f"vn{first}")
                 nc.scalar.activation(vn[:], norm2[piece][:], ACT.Sqrt, bias=eps[:])
                 s_psum[piece] = psum.tile([P, width], F32, name="s_psum")
                 nc.tensor.matmul(s_psum[piece][:], norm_weights[:], vn[:], start=True, stop=vector_is_free)
@@ -93,7 +92,7 @@ def tile_messagefunction_kernel(tc, x, other, w_norm, b_scalar, w_gate, b_gate, 
 
             for piece in group:
                 first, width = piece
-                s_bf16 = work.tile([P, width], BF16, name=f"s_bf16_{width}")
+                s_bf16 = held.tile([P, width], BF16, name=f"s_bf16_{first}")
                 if vector_is_free:
                     s_no_bias[piece] = s_sum[:, first - LAST_GROUP[0][0] : first - LAST_GROUP[0][0] + width]
                     nc.vector.tensor_tensor(s_no_bias[piece], s_psum[piece][:], sp[piece], ADD)

@@ -107,6 +107,12 @@ def tile_messagefunction_kernel(tc, x, other, w_norm, b_scalar, w_gate, b_gate, 
                 gate[piece] = held.tile([P, width], F32, name=f"gate{first}")
                 nc.scalar.activation(gate[piece][:], gate_psum[piece][:], ACT.Sigmoid, bias=gate_bias[:])
 
+            if group is FIRST_GROUP:
+                s_relu_first = held.tile([P, 2 * BANK], F32, name="s_relu_first")
+                for first, width in FIRST_GROUP:
+                    nc.scalar.activation(s_relu_first[:, first : first + width], s_no_bias[first, width], ACT.Relu, bias=scalar_bias[:])
+                nc.sync.dma_start(out[0:P, 0 : 2 * BANK], s_relu_first[:])
+
         for piece in PIECES:
             first, width = piece
             gated = held.tile([P, 3, width], F32, name=f"gated{first}")
@@ -114,10 +120,6 @@ def tile_messagefunction_kernel(tc, x, other, w_norm, b_scalar, w_gate, b_gate, 
             nc.vector.tensor_tensor(gated[:], vh[piece][:], gate_for_all, MULT)
             nc.sync.dma_start(out[P : 4 * P, first : first + width].rearrange("(r p) j -> p r j", p=P), gated[:])
 
-        s_relu_first = held.tile([P, 2 * BANK], F32, name="s_relu_first")
-        for first, width in FIRST_GROUP:
-            nc.scalar.activation(s_relu_first[:, first : first + width], s_no_bias[first, width], ACT.Relu, bias=scalar_bias[:])
-        nc.sync.dma_start(out[0:P, 0 : 2 * BANK], s_relu_first[:])
         s_relu_last = held.tile([P, 2 * BANK], F32, name="s_relu_last")
         nc.vector.tensor_scalar(s_relu_last[:], s_sum[:], scalar_bias[:], 0.0, ADD, MAX)
         nc.sync.dma_start(out[0:P, 2 * BANK : EDGES], s_relu_last[:])

import concourse.mybir as mybir
from concourse.masks import make_identity

F32, BF16, U16 = mybir.dt.float32, mybir.dt.bfloat16, mybir.dt.uint16
ADD, MULT, MAX = mybir.AluOpType.add, mybir.AluOpType.mult, mybir.AluOpType.max
ACT = mybir.ActivationFunctionType

P = 128
NODES = 512
EDGES = 2048
BANK = 512
EPS = 1e-8

FIRST_GROUP = [(0, BANK), (BANK, BANK)]
LAST_GROUP = [(2 * BANK + i * BANK // 2, BANK // 2) for i in range(4)]
LAST_GROUP_WIDE = [(2 * BANK, BANK), (3 * BANK, BANK)]
PIECES = FIRST_GROUP + LAST_GROUP

FLOPS = 2 * 2 * P * P * EDGES


def tile_messagefunction_kernel(tc, x, other, w_norm, b_scalar, w_gate, b_gate, offs, out):
    nc = tc.nc
    with (
        tc.tile_pool(name="held", bufs=1) as held,
        tc.psum_pool(name="psum", bufs=4) as psum,
    ):
        offsets = held.tile([P, EDGES // 16], U16, name="offsets")
        nc.sync.dma_start(offsets[:], offs)

        identity = held.tile([P, P], F32, name="identity")
        make_identity(nc, identity[:])
        eps = held.tile([P, 1], F32, name="eps")
        nc.gpsimd.memset(eps[:], EPS)
        table_set_warmer = held.tile([P, 1], F32, name="table_set_warmer")
        nc.scalar.activation(table_set_warmer[:], eps[:], ACT.Sqrt)

        norm_weights = held.tile([P, P], BF16, name="norm_weights")
        gate_weights = held.tile([P, P], BF16, name="gate_weights")
        scalar_bias = held.tile([P, 1], F32, name="scalar_bias")
        gate_bias = held.tile([P, 1], F32, name="gate_bias")

        tables = {}

        def look_up_and_add(b, piece, a):
            first, width = piece
            if b not in tables:
                tables[b] = held.tile([P, NODES], F32, name=f"table{b}")
                nc.sync.dma_start(tables[b][:], x[b * P : (b + 1) * P, :])
            term = held.tile([P, width], F32, name=f"term{b}_{first}")
            nc.sync.dma_start(term[:], other[b * P : (b + 1) * P, first : first + width])
            nc.vector.tensor_tensor(a, tables[b][:].indirect(offsets[:, first // 16 : (first + width) // 16]), term[:], ADD)

        vh, norm2, s_psum, sp, s_no_bias, gate_psum, gate = {}, {}, {}, {}, {}, {}, {}
        s_sum = held.tile([P, 2 * BANK], F32, name="s_sum")
        for group in (FIRST_GROUP, LAST_GROUP):
            vector_is_free = group is LAST_GROUP

            for piece in group:
                first, width = piece
                vh[piece] = held.tile([P, 3, width], F32, name=f"vh{first}")
                for r in range(3):
                    look_up_and_add(1 + r, piece, vh[piece][:, r, :])
                if first == 0:
                    nc.sync.dma_start(norm_weights[:], w_norm)
                    nc.sync.dma_start(scalar_bias[:], b_scalar)
                    nc.sync.dma_start(gate_weights[:], w_gate)
                    nc.sync.dma_start(gate_bias[:], b_gate)
                norm2[piece] = psum.tile([P, width], F32, name="norm2", tag="read_once")
                for r in range(3):
                    squared = held.tile([P, width], F32, name=f"squared{r}_{first}")
                    nc.scalar.activation(squared[:], vh[piece][:, r, :], ACT.Square)
                    nc.tensor.matmul(norm2[piece][:], identity[:], squared[:], start=(r == 0), stop=(r == 2))

            for piece in group:
                first, width = piece
                vn = held.tile([P, width], BF16, name=f"vn{first}")
                nc.scalar.activation(vn[:], norm2[piece][:], ACT.Sqrt, bias=eps[:])
                s_psum[piece] = psum.tile([P, width], F32, name="s_psum")
                nc.tensor.matmul(s_psum[piece][:], norm_weights[:], vn[:], start=True, stop=vector_is_free)

            for wide in FIRST_GROUP if group is FIRST_GROUP else LAST_GROUP_WIDE:
                sp_wide = held.tile([P, BANK], F32, name=f"sp{wide[0]}")
                look_up_and_add(0, wide, sp_wide[:])
                for piece in group:
                    if wide[0] <= piece[0] < wide[0] + BANK:
                        sp[piece] = sp_wide[:, piece[0] - wide[0] : piece[0] - wide[0] + piece[1]]
            for piece in group:
                if not vector_is_free:
                    nc.tensor.matmul(s_psum[piece][:], identity[:], sp[piece], start=False, stop=True)
                    s_no_bias[piece] = s_psum[piece][:]

            for piece in group:
                first, width = piece
                s_bf16 = held.tile([P, width], BF16, name=f"s_bf16_{first}")
                if vector_is_free:
                    s_no_bias[piece] = s_sum[:, first - LAST_GROUP[0][0] : first - LAST_GROUP[0][0] + width]
                    nc.vector.tensor_tensor(s_no_bias[piece], s_psum[piece][:], sp[piece], ADD)
                    nc.vector.tensor_scalar_add(s_bf16[:], s_no_bias[piece], scalar_bias[:])
                else:
                    nc.scalar.activation(s_bf16[:], s_psum[piece][:], ACT.Identity, bias=scalar_bias[:])
                gate_psum[piece] = psum.tile([P, width], F32, name="gate_psum", tag="read_once")
                nc.tensor.matmul(gate_psum[piece][:], gate_weights[:], s_bf16[:], start=True, stop=True)

            for piece in group:
                first, width = piece
                gate[piece] = held.tile([P, width], F32, name=f"gate{first}")
                nc.scalar.activation(gate[piece][:], gate_psum[piece][:], ACT.Sigmoid, bias=gate_bias[:])

            if group is FIRST_GROUP:
                s_relu_first = held.tile([P, 2 * BANK], F32, name="s_relu_first")
                for first, width in FIRST_GROUP:
                    nc.scalar.activation(s_relu_first[:, first : first + width], s_no_bias[first, width], ACT.Relu, bias=scalar_bias[:])
                nc.sync.dma_start(out[0:P, 0 : 2 * BANK], s_relu_first[:])

        for piece in PIECES:
            first, width = piece
            gated = held.tile([P, 3, width], F32, name=f"gated{first}")
            gate_for_all = gate[piece][:].unsqueeze(1).to_broadcast([P, 3, width])
            nc.vector.tensor_tensor(gated[:], vh[piece][:], gate_for_all, MULT)
            nc.sync.dma_start(out[P : 4 * P, first : first + width].rearrange("(r p) j -> p r j", p=P), gated[:])

        s_relu_last = held.tile([P, 2 * BANK], F32, name="s_relu_last")
        nc.vector.tensor_scalar(s_relu_last[:], s_sum[:], scalar_bias[:], 0.0, ADD, MAX)
        nc.sync.dma_start(out[0:P, 2 * BANK : EDGES], s_relu_last[:])
